import numpy as np
import ml_dtypes


def mxq(x, axis, fmt="e4m3"):
    dtype, down = {"e4m3": (ml_dtypes.float8_e4m3fn, 7), "e5m2": (ml_dtypes.float8_e5m2, 14)}[fmt]
    v = np.moveaxis(np.asarray(x, np.float32).astype(ml_dtypes.bfloat16).astype(np.float64), axis, -1)
    blocks = v.reshape(v.shape[:-1] + (-1, 32))
    amax = np.abs(blocks).max(-1, keepdims=True)
    byte = np.maximum(np.where(amax > 0, np.frexp(amax)[1] - 1 + 127, 0) - down, 1)
    scale = np.exp2(byte - 127.0)
    codes = (blocks / scale).astype(np.float32).astype(dtype).astype(np.float64)
    return np.moveaxis((codes * scale).reshape(v.shape), -1, axis)


WIDE = False


def mx_kscale(k):
    if not WIDE:
        return np.ones(k)
    levels = np.array([10, -10, 5, -5, 0])
    a = np.random.permutation(np.resize(levels, k // 512 * 4)).reshape(k // 512, 4)
    idx = np.arange(k)
    return np.exp2(a[idx // 512, idx % 128 // 32])


BF16 = ml_dtypes.bfloat16


def bf(x):
    return np.asarray(x, np.float32).astype(BF16)


def f64(x):
    return np.asarray(x).astype(np.float64)


B, E, D, H = 1024, 8, 128, 512
FACTOR = 1.0


def swish(v):
    return v / (1.0 + np.exp(-v))


def setup_inputs():
    s = mx_kscale(H)
    return {"h2": bf(swish(np.random.standard_normal((B, E, H)) * 1.5) * s),
            "W3": bf(np.random.standard_normal((E, H, H)) * 1.5 / np.sqrt(H) / s[:, None]),
            "b3": bf(np.random.standard_normal((E, H)) * 0.3),
            "W4": bf(np.random.standard_normal((E, H, D)) / np.sqrt(H)),
            "b4": bf(np.random.standard_normal((E, D)) * 0.3)}


def reference(h2, W3, b3, W4, b4):
    x = f64(h2).transpose(1, 0, 2)
    h3 = swish((mxq(x, 2, "e4m3") @ mxq(f64(W3), 1, "e4m3")) + f64(b3)[:, None, :])
    out = ((mxq(h3, 2, "e4m3") @ mxq(f64(W4), 1, "e4m3")) + f64(b4)[:, None, :]) * FACTOR
    return out.transpose(1, 0, 2).reshape(-1, D)

@@ -1,0 +1,268 @@
+from contextlib import ExitStack
+
+import concourse.mybir as mybir
+from concourse.masks import make_identity
+
+F32 = mybir.dt.float32
+BF16 = mybir.dt.bfloat16
+U32 = mybir.dt.uint32
+U8 = mybir.dt.uint8
+FP8X4 = mybir.dt.float8_e4m3fn_x4
+SILU = mybir.ActivationFunctionType.Silu
+ADD = mybir.AluOpType.add
+
+B, E, D, H = 1024, 8, 128, 512
+P = 128
+PACK = 4
+TOK = 512
+CHUNKS = TOK // P
+HALVES = B // TOK
+UNITS = E * HALVES
+FLOPS = 2 * B * E * H * (H + D)
+
+PIN = True
+
+
+def tile_environvectorfield_pb_t_kernel(tc, h2, W3, b3, W4, b4, out):
+    nc = tc.nc
+    h2_v = h2.rearrange("(h c p) e k -> e h p c k", h=HALVES, c=CHUNKS, p=P)
+    w3_v = W3.rearrange("e (u q r) n -> e q u (r n)", u=2, q=P, r=2)
+    w4_v = W4.rearrange("e (t p) d -> p (e t) d", t=PACK, p=P)
+    b3_v = b3.rearrange("e (m p) -> (e m) p", p=P)
+    b4_v = b4.rearrange("e d -> (e d)").partition_broadcast(P)
+    out_v = out.rearrange("(h c p e) d -> e h p c d", h=HALVES, c=CHUNKS, p=P, e=E)
+
+    with ExitStack() as ctx:
+        keep = ctx.enter_context(tc.tile_pool(name="keep", bufs=1))
+        ring = ctx.enter_context(tc.tile_pool(name="ring", bufs=2))
+        ps_t = ctx.enter_context(tc.psum_pool(name="ps_t", bufs=2))
+        ps_z = ctx.enter_context(tc.psum_pool(name="ps_z", bufs=4))
+        ps_o = ctx.enter_context(tc.psum_pool(name="ps_o", bufs=2))
+        if PIN:
+            ctx.enter_context(tc.manual_schedule())
+
+        ident = keep.tile([P, P], F32, name="ident")
+        make_identity(nc, ident[:])
+        b3_rows = keep.tile([P, P], BF16, name="b3_rows")
+        nc.vector.memset(b3_rows[:], 0.0)
+        nc.sync.dma_start(out=b3_rows[0 : E * PACK, :], in_=b3_v)
+
+        warm = keep.tile([P, 1], F32, name="warm")
+        nc.vector.memset(warm[:], 0.0)
+        warm_out = keep.tile([P, 1], F32, name="warm_out")
+        nc.scalar.activation(out=warm_out[:], in_=warm[:], func=SILU)
+
+        x_raw = {}
+        w_raw = {}
+
+        def load_x(u):
+            t = keep.tile([P, CHUNKS * H], BF16, name="x_raw%d" % u)
+            nc.sync.dma_start(
+                out=t[:].rearrange("p (c k) -> p c k", c=CHUNKS), in_=h2_v[u // HALVES, u % HALVES]
+            )
+            x_raw[u] = t
+
+        def load_w(e):
+            t = keep.tile([P, PACK * H], BF16, name="w_raw%d" % e)
+            nc.sync.dma_start(out=t[:].rearrange("q (u r) -> q u r", u=2), in_=w3_v[e])
+            w_raw[e] = t
+
+        w4_raw = keep.tile([P, E * PACK * D], BF16, name="w4_raw")
+        b4_all = keep.tile([P, E * D], BF16, name="b4_all")
+
+        load_x(0)
+        load_w(0)
+        load_x(1)
+        load_w(1)
+        load_x(2)
+        nc.sync.dma_start(out=w4_raw[:].rearrange("p (g d) -> p g d", d=D), in_=w4_v)
+        nc.sync.dma_start(out=b4_all[:], in_=b4_v)
+        load_x(3)
+        for s in range(1, UNITS):
+            if s + 3 < UNITS:
+                load_x(s + 3)
+            if s % 2 == 1 and (s + 3) // 2 < E:
+                load_w((s + 3) // 2)
+
+        b3_f = keep.tile([P, P], F32, name="b3_f")
+        nc.vector.tensor_copy(out=b3_f[:], in_=b3_rows[:])
+        b3_ps = ps_t.tile([P, 4, P], F32, name="tp", tag="tp")
+        nc.tensor.transpose(b3_ps[:, 0, :], b3_f[:], ident[:])
+        b3_t = keep.tile([P, E * PACK], F32, name="b3_t")
+        nc.vector.tensor_copy(out=b3_t[:], in_=b3_ps[:, 0, 0 : E * PACK])
+
+        tp = {}
+        xg = {}
+        xq = {}
+        wg = {}
+        wq = {}
+        zt = {}
+        hr = {}
+        hg = {}
+        hq = {}
+        ot = {}
+
+        def transposes(u):
+            words = x_raw[u][:].bitcast(F32)
+            banks = []
+            for j in range(2):
+                bank = ps_t.tile([P, 4, P], F32, name="tp", tag="tp")
+                for s in range(4):
+                    col = 256 * (2 * j + s // 2) + P * (s % 2)
+                    nc.tensor.transpose(bank[:, s, :], words[:, col : col + P], ident[:])
+                banks.append(bank)
+            tp[u] = banks
+
+        def evacuate(u):
+            g = ring.tile([P, PACK * TOK], BF16, name="xg", tag="xg", bufs=3, align_bytes=64)
+            words = g[:].bitcast(F32).rearrange("p (c b w) -> p c b w", c=CHUNKS, w=2)
+            for j in range(2):
+                nc.scalar.copy(
+                    out=words[:, 2 * j : 2 * j + 2],
+                    in_=tp[u][j][:].rearrange("p (c w) b -> p c b w", w=2),
+                )
+            xg[u] = g
+
+        def quantise(src, width, tag, bufs, pool):
+            codes = pool.tile([P, width], U32, name=tag + "c", tag=tag + "c", bufs=bufs, align_bytes=64)
+            scales = pool.tile([P, width], U8, name=tag + "s", tag=tag + "s", bufs=bufs, align_bytes=64)
+            nc.vector.quantize_mx(out=codes[:].bitcast(FP8X4), scales=scales[:], in_=src)
+            return (codes, scales)
+
+        def quantise_x(u):
+            xq[u] = quantise(xg[u][:], TOK, "xq", 3, ring)
+
+        def regroup(dst, src):
+            nc.vector.tensor_copy(
+                out=dst.rearrange("p (c i t) -> p c t i", i=4, t=PACK),
+                in_=src.rearrange("p (t c i) -> p c t i", t=PACK, i=4),
+            )
+
+        def regroup_w(e):
+            g = ring.tile([P, PACK * H], BF16, name="wg", tag="wg", bufs=2, align_bytes=64)
+            regroup(g[:], w_raw[e][:])
+            wg[e] = g
+
+        def quantise_w(e):
+            wq[e] = quantise(wg[e][:], H, "wq%d" % e, 1, keep)
+
+        def layer1(u, m):
+            z = ps_z.tile([P, TOK], F32, name="z", tag="z")
+            wc, ws = wq[u // HALVES]
+            xc, xs = xq[u]
+            nc.tensor.matmul_mx(
+                out=z[:],
+                lhsT=wc[:, P * m : P * m + P].bitcast(FP8X4),
+                lhsT_scale=ws[:, P * m : P * m + P],
+                rhs=xc[:].bitcast(FP8X4),
+                rhs_scale=xs[:],
+                start=True,
+                stop=True,
+            )
+            zt[(u, m)] = z
+
+        def swish(u, m):
+            if m == 0:
+                hr[u] = ring.tile([P, PACK * TOK], BF16, name="hr", tag="hr", bufs=3)
+            col = PACK * (u // HALVES) + m
+            nc.scalar.activation(
+                out=hr[u][:, TOK * m : TOK * m + TOK],
+                in_=zt[(u, m)][:],
+                func=SILU,
+                bias=b3_t[:, col : col + 1],
+                scale=1.0,
+            )
+
+        def regroup_h(u):
+            g = ring.tile([P, PACK * TOK], BF16, name="hg", tag="hg", bufs=2, align_bytes=64)
+            regroup(g[:], hr[u][:])
+            hg[u] = g
+
+        def quantise_h(u):
+            hq[u] = quantise(hg[u][:], TOK, "hq", 3, ring)
+
+        w4g = keep.tile([P, E * PACK * D], BF16, name="w4g", align_bytes=64)
+        w4q = []
+
+        def regroup_w4(half):
+            lo = half * (E // 2) * PACK * D
+            hi = lo + (E // 2) * PACK * D
+            nc.vector.tensor_copy(
+                out=w4g[:, lo:hi].rearrange("p (e d t) -> p e d t", d=D, t=PACK),
+                in_=w4_raw[:, lo:hi].rearrange("p (e t d) -> p e d t", t=PACK, d=D),
+            )
+
+        def quantise_w4():
+            w4q.append(quantise(w4g[:], E * D, "w4q", 1, keep))
+
+        def layer2(u):
+            o = ps_o.tile([P, CHUNKS, D], F32, name="o", tag="o")
+            e = u // HALVES
+            hc, hs = hq[u]
+            wc, ws = w4q[0]
+            for c in range(CHUNKS):
+                nc.tensor.matmul_mx(
+                    out=o[:, c, :],
+                    lhsT=hc[:, P * c : P * c + P].bitcast(FP8X4),
+                    lhsT_scale=hs[:, P * c : P * c + P],
+                    rhs=wc[:, D * e : D * e + D].bitcast(FP8X4),
+                    rhs_scale=ws[:, D * e : D * e + D],
+                    start=True,
+                    stop=True,
+                )
+            ot[u] = o
+
+        def finish(u):
+            e = u // HALVES
+            res = ring.tile([P, CHUNKS, D], F32, name="res", tag="res", bufs=8)
+            nc.vector.tensor_tensor(
+                out=res[:],
+                in0=ot[u][:],
+                in1=b4_all[:, D * e : D * e + D].unsqueeze(1).to_broadcast([P, CHUNKS, D]),
+                op=ADD,
+            )
+            nc.sync.dma_start(out=out_v[e, u % HALVES], in_=res[:])
+
+        transposes(0)
+        evacuate(0)
+        regroup_w(0)
+        quantise_x(0)
+        quantise_w(0)
+        for m in range(PACK):
+            layer1(0, m)
+        transposes(1)
+        evacuate(1)
+        transposes(2)
+        regroup_w(1)
+
+        for s in range(UNITS + 1):
+            if s + 1 < UNITS:
+                quantise_x(s + 1)
+            if s == 0:
+                quantise_w(1)
+            if s < UNITS:
+                for m in range(PACK):
+                    swish(s, m)
+                    if s + 1 < UNITS:
+                        layer1(s + 1, m)
+            if s + 2 < UNITS:
+                evacuate(s + 2)
+            if s == 0:
+                regroup_w4(0)
+                regroup_w4(1)
+                quantise_w4()
+            if s >= 1:
+                regroup_h(s - 1)
+            if 2 <= s < UNITS + 1 and s - 2 < UNITS - 2:
+                finish(s - 2)
+            if s >= 1:
+                quantise_h(s - 1)
+                layer2(s - 1)
+            if s + 3 < UNITS:
+                transposes(s + 3)
+            if s >= UNITS - 1:
+                finish(s - 1)
+            if s >= 1 and s % 2 == 1 and (s + 3) // 2 < E:
+                regroup_w((s + 3) // 2)
+            if s >= 2 and s % 2 == 0 and (s + 2) // 2 < E:
+                quantise_w((s + 2) // 2)

@@ -15,22 +15,35 @@ B, E, D, H = 1024, 8, 128, 512
 P = 128
 PACK = 4
 TOK = 512
-CHUNKS = TOK // P
-HALVES = B // TOK
-UNITS = E * HALVES
+WCOLS = H + D
 FLOPS = 2 * B * E * H * (H + D)
 
-PIN = True
+PIN = False
+FIRST = [256,256,512]
+LAST = [512,256,256]
+ACT_WR = [3,5]
+W_LEAD = 1
 
 
 def tile_environvectorfield_pb_t_kernel(tc, h2, W3, b3, W4, b4, out):
     nc = tc.nc
-    h2_v = h2.rearrange("(h c p) e k -> e h p c k", h=HALVES, c=CHUNKS, p=P)
-    w3_v = W3.rearrange("e (u q r) n -> e q u (r n)", u=2, q=P, r=2)
-    w4_v = W4.rearrange("e (t p) d -> p (e t) d", t=PACK, p=P)
+    units = []
+    for e in range(E):
+        sizes = FIRST if e == 0 else (LAST if e == E - 1 else [TOK, TOK])
+        t0 = 0
+        for n in sizes:
+            units.append((e, t0, n))
+            t0 += n
+    n_units = len(units)
+    first_unit = {}
+    for u in range(n_units):
+        if units[u][0] not in first_unit:
+            first_unit[units[u][0]] = u
+
+    w4_v = W4.rearrange("e (t p) d -> e p t d", t=PACK, p=P)
     b3_v = b3.rearrange("e (m p) -> (e m) p", p=P)
     b4_v = b4.rearrange("e d -> (e d)").partition_broadcast(P)
-    out_v = out.rearrange("(h c p e) d -> e h p c d", h=HALVES, c=CHUNKS, p=P, e=E)
+    out_v = out.rearrange("(b e) d -> e b d", e=E)
 
     with ExitStack() as ctx:
         keep = ctx.enter_context(tc.tile_pool(name="keep", bufs=1))
@@ -46,7 +59,6 @@ def tile_environvectorfield_pb_t_kernel(tc, h2, W3, b3, W4, b4, out):
         b3_rows = keep.tile([P, P], BF16, name="b3_rows")
         nc.vector.memset(b3_rows[:], 0.0)
         nc.sync.dma_start(out=b3_rows[0 : E * PACK, :], in_=b3_v)
-
         warm = keep.tile([P, 1], F32, name="warm")
         nc.vector.memset(warm[:], 0.0)
         warm_out = keep.tile([P, 1], F32, name="warm_out")
@@ -56,33 +68,36 @@ def tile_environvectorfield_pb_t_kernel(tc, h2, W3, b3, W4, b4, out):
         w_raw = {}
 
         def load_x(u):
-            t = keep.tile([P, CHUNKS * H], BF16, name="x_raw%d" % u)
+            e, t0, n = units[u]
+            t = keep.tile([P, (n // P) * H], BF16, name="x_raw%d" % u)
             nc.sync.dma_start(
-                out=t[:].rearrange("p (c k) -> p c k", c=CHUNKS), in_=h2_v[u // HALVES, u % HALVES]
+                out=t[:].rearrange("p (c k) -> p c k", k=H),
+                in_=h2[t0 : t0 + n, e, :].rearrange("(c p) k -> p c k", p=P),
             )
             x_raw[u] = t
 
         def load_w(e):
-            t = keep.tile([P, PACK * H], BF16, name="w_raw%d" % e)
-            nc.sync.dma_start(out=t[:].rearrange("q (u r) -> q u r", u=2), in_=w3_v[e])
+            t = keep.tile([P, PACK, WCOLS], BF16, name="w_raw%d" % e)
+            for half in range(2):
+                nc.sync.dma_start(
+                    out=t[:, 2 * half : 2 * half + 2, 0:H],
+                    in_=W3[e, 256 * half : 256 * half + 256, :].rearrange("(q r) n -> q r n", r=2),
+                )
+            nc.sync.dma_start(out=t[:, :, H:WCOLS], in_=w4_v[e])
             w_raw[e] = t
 
-        w4_raw = keep.tile([P, E * PACK * D], BF16, name="w4_raw")
         b4_all = keep.tile([P, E * D], BF16, name="b4_all")
 
-        load_x(0)
-        load_w(0)
-        load_x(1)
-        load_w(1)
-        load_x(2)
-        nc.sync.dma_start(out=w4_raw[:].rearrange("p (g d) -> p g d", d=D), in_=w4_v)
-        nc.sync.dma_start(out=b4_all[:], in_=b4_v)
-        load_x(3)
-        for s in range(1, UNITS):
-            if s + 3 < UNITS:
-                load_x(s + 3)
-            if s % 2 == 1 and (s + 3) // 2 < E:
-                load_w((s + 3) // 2)
+        w_at = {}
+        for e in range(E):
+            at = max(0, first_unit[e] - W_LEAD)
+            w_at[at] = w_at.get(at, []) + [e]
+        for u in range(n_units):
+            load_x(u)
+            for e in w_at.get(u, []):
+                load_w(e)
+            if u == 3:
+                nc.sync.dma_start(out=b4_all[:], in_=b4_v)
 
         b3_f = keep.tile([P, P], F32, name="b3_f")
         nc.vector.tensor_copy(out=b3_f[:], in_=b3_rows[:])
@@ -96,6 +111,7 @@ def tile_environvectorfield_pb_t_kernel(tc, h2, W3, b3, W4, b4, out):
         xq = {}
         wg = {}
         wq = {}
+        w4q = {}
         zt = {}
         hr = {}
         hg = {}
@@ -103,9 +119,10 @@ def tile_environvectorfield_pb_t_kernel(tc, h2, W3, b3, W4, b4, out):
         ot = {}
 
         def transposes(u):
+            n = units[u][2]
             words = x_raw[u][:].bitcast(F32)
             banks = []
-            for j in range(2):
+            for j in range(n // 256):
                 bank = ps_t.tile([P, 4, P], F32, name="tp", tag="tp")
                 for s in range(4):
                     col = 256 * (2 * j + s // 2) + P * (s % 2)
@@ -115,154 +132,157 @@ def tile_environvectorfield_pb_t_kernel(tc, h2, W3, b3, W4, b4, out):
 
         def evacuate(u):
             g = ring.tile([P, PACK * TOK], BF16, name="xg", tag="xg", bufs=3, align_bytes=64)
-            words = g[:].bitcast(F32).rearrange("p (c b w) -> p c b w", c=CHUNKS, w=2)
-            for j in range(2):
+            words = g[:].bitcast(F32).rearrange("p (c b w) -> p c b w", b=P, w=2)
+            for j in range(len(tp[u])):
                 nc.scalar.copy(
                     out=words[:, 2 * j : 2 * j + 2],
                     in_=tp[u][j][:].rearrange("p (c w) b -> p c b w", w=2),
                 )
             xg[u] = g
 
-        def quantise(src, width, tag, bufs, pool):
-            codes = pool.tile([P, width], U32, name=tag + "c", tag=tag + "c", bufs=bufs, align_bytes=64)
-            scales = pool.tile([P, width], U8, name=tag + "s", tag=tag + "s", bufs=bufs, align_bytes=64)
-            nc.vector.quantize_mx(out=codes[:].bitcast(FP8X4), scales=scales[:], in_=src)
+        def quantise(src, width, full, tag, bufs, pool):
+            codes = pool.tile([P, full], U32, name=tag + "c", tag=tag + "c", bufs=bufs, align_bytes=64)
+            scales = pool.tile([P, full], U8, name=tag + "s", tag=tag + "s", bufs=bufs, align_bytes=64)
+            nc.vector.quantize_mx(
+                out=codes[:, 0:width].bitcast(FP8X4), scales=scales[:, 0:width], in_=src
+            )
             return (codes, scales)
 
         def quantise_x(u):
-            xq[u] = quantise(xg[u][:], TOK, "xq", 3, ring)
-
-        def regroup(dst, src):
-            nc.vector.tensor_copy(
-                out=dst.rearrange("p (c i t) -> p c t i", i=4, t=PACK),
-                in_=src.rearrange("p (t c i) -> p c t i", t=PACK, i=4),
-            )
+            n = units[u][2]
+            xq[u] = quantise(xg[u][:, 0 : PACK * n], n, TOK, "xq", 3, ring)
 
         def regroup_w(e):
-            g = ring.tile([P, PACK * H], BF16, name="wg", tag="wg", bufs=2, align_bytes=64)
-            regroup(g[:], w_raw[e][:])
+            g = ring.tile([P, PACK * WCOLS], BF16, name="wg", tag="wg", bufs=2, align_bytes=64)
+            dst = g[:].rearrange("p (c i t) -> p c t i", i=4, t=PACK)
+            src = w_raw[e][:].rearrange("p t (c i) -> p c t i", i=4)
+            if e in ACT_WR:
+                nc.scalar.copy(out=dst, in_=src)
+            else:
+                nc.vector.tensor_copy(out=dst, in_=src)
             wg[e] = g
 
         def quantise_w(e):
-            wq[e] = quantise(wg[e][:], H, "wq%d" % e, 1, keep)
+            wq[e] = quantise(wg[e][:, 0 : PACK * H], H, H, "wq%d" % e, 1, keep)
+            w4q[e] = quantise(wg[e][:, PACK * H : PACK * WCOLS], D, D, "w4q%d" % e, 1, keep)
 
         def layer1(u, m):
+            e, t0, n = units[u]
             z = ps_z.tile([P, TOK], F32, name="z", tag="z")
-            wc, ws = wq[u // HALVES]
+            wc, ws = wq[e]
             xc, xs = xq[u]
             nc.tensor.matmul_mx(
-                out=z[:],
+                out=z[:, 0:n],
                 lhsT=wc[:, P * m : P * m + P].bitcast(FP8X4),
                 lhsT_scale=ws[:, P * m : P * m + P],
-                rhs=xc[:].bitcast(FP8X4),
-                rhs_scale=xs[:],
+                rhs=xc[:, 0:n].bitcast(FP8X4),
+                rhs_scale=xs[:, 0:n],
                 start=True,
                 stop=True,
             )
             zt[(u, m)] = z
 
         def swish(u, m):
+            e, t0, n = units[u]
             if m == 0:
-                hr[u] = ring.tile([P, PACK * TOK], BF16, name="hr", tag="hr", bufs=3)
-            col = PACK * (u // HALVES) + m
+                hr[u] = ring.tile([P, PACK, TOK], BF16, name="hr", tag="hr", bufs=3)
+            col = PACK * e + m
             nc.scalar.activation(
-                out=hr[u][:, TOK * m : TOK * m + TOK],
-                in_=zt[(u, m)][:],
+                out=hr[u][:, m, 0:n],
+                in_=zt[(u, m)][:, 0:n],
                 func=SILU,
                 bias=b3_t[:, col : col + 1],
                 scale=1.0,
             )
 
         def regroup_h(u):
+            n = units[u][2]
             g = ring.tile([P, PACK * TOK], BF16, name="hg", tag="hg", bufs=2, align_bytes=64)
-            regroup(g[:], hr[u][:])
+            nc.vector.tensor_copy(
+                out=g[:, 0 : PACK * n].rearrange("p (c i t) -> p c t i", i=4, t=PACK),
+                in_=hr[u][:, :, 0:n].rearrange("p t (c i) -> p c t i", i=4),
+            )
             hg[u] = g
 
         def quantise_h(u):
-            hq[u] = quantise(hg[u][:], TOK, "hq", 3, ring)
-
-        w4g = keep.tile([P, E * PACK * D], BF16, name="w4g", align_bytes=64)
-        w4q = []
-
-        def regroup_w4(half):
-            lo = half * (E // 2) * PACK * D
-            hi = lo + (E // 2) * PACK * D
-            nc.vector.tensor_copy(
-                out=w4g[:, lo:hi].rearrange("p (e d t) -> p e d t", d=D, t=PACK),
-                in_=w4_raw[:, lo:hi].rearrange("p (e t d) -> p e d t", t=PACK, d=D),
-            )
-
-        def quantise_w4():
-            w4q.append(quantise(w4g[:], E * D, "w4q", 1, keep))
+            n = units[u][2]
+            hq[u] = quantise(hg[u][:, 0 : PACK * n], n, TOK, "hq", 3, ring)
 
         def layer2(u):
-            o = ps_o.tile([P, CHUNKS, D], F32, name="o", tag="o")
-            e = u // HALVES
+            e, t0, n = units[u]
+            o = ps_o.tile([P, TOK // P, D], F32, name="o", tag="o")
             hc, hs = hq[u]
-            wc, ws = w4q[0]
-            for c in range(CHUNKS):
+            wc, ws = w4q[e]
+            for c in range(n // P):
                 nc.tensor.matmul_mx(
                     out=o[:, c, :],
                     lhsT=hc[:, P * c : P * c + P].bitcast(FP8X4),
                     lhsT_scale=hs[:, P * c : P * c + P],
-                    rhs=wc[:, D * e : D * e + D].bitcast(FP8X4),
-                    rhs_scale=ws[:, D * e : D * e + D],
+                    rhs=wc[:].bitcast(FP8X4),
+                    rhs_scale=ws[:],
                     start=True,
                     stop=True,
                 )
             ot[u] = o
 
         def finish(u):
-            e = u // HALVES
-            res = ring.tile([P, CHUNKS, D], F32, name="res", tag="res", bufs=8)
+            e, t0, n = units[u]
+            nch = n // P
+            res = ring.tile([P, TOK // P, D], F32, name="res", tag="res", bufs=8)
             nc.vector.tensor_tensor(
-                out=res[:],
-                in0=ot[u][:],
-                in1=b4_all[:, D * e : D * e + D].unsqueeze(1).to_broadcast([P, CHUNKS, D]),
+                out=res[:, 0:nch, :],
+                in0=ot[u][:, 0:nch, :],
+                in1=b4_all[:, D * e : D * e + D].unsqueeze(1).to_broadcast([P, nch, D]),
                 op=ADD,
             )
-            nc.sync.dma_start(out=out_v[e, u % HALVES], in_=res[:])
+            nc.sync.dma_start(
+                out=out_v[e, t0 : t0 + n, :].rearrange("(c p) d -> p c d", p=P), in_=res[:, 0:nch, :]
+            )
+
+        wr_at = {}
+        qw_at = {}
+        for e in range(1, E):
+            use = first_unit[e] - 1
+            wr_at[max(-1, use - W_LEAD - 1)] = wr_at.get(max(-1, use - W_LEAD - 1), []) + [e]
+            qw_at[max(-1, use - W_LEAD)] = qw_at.get(max(-1, use - W_LEAD), []) + [e]
 
         transposes(0)
         evacuate(0)
         regroup_w(0)
         quantise_x(0)
         quantise_w(0)
+        transposes(1)
         for m in range(PACK):
             layer1(0, m)
-        transposes(1)
         evacuate(1)
         transposes(2)
-        regroup_w(1)
+        for e in wr_at.get(-1, []):
+            regroup_w(e)
+        for e in qw_at.get(-1, []):
+            quantise_w(e)
 
-        for s in range(UNITS + 1):
-            if s + 1 < UNITS:
+        for s in range(n_units + 1):
+            if s + 1 < n_units:
                 quantise_x(s + 1)
-            if s == 0:
-                quantise_w(1)
-            if s < UNITS:
+            if s < n_units:
                 for m in range(PACK):
                     swish(s, m)
-                    if s + 1 < UNITS:
+                    if s + 1 < n_units:
                         layer1(s + 1, m)
-            if s + 2 < UNITS:
+            if s + 2 < n_units:
                 evacuate(s + 2)
-            if s == 0:
-                regroup_w4(0)
-                regroup_w4(1)
-                quantise_w4()
             if s >= 1:
                 regroup_h(s - 1)
-            if 2 <= s < UNITS + 1 and s - 2 < UNITS - 2:
+            if 2 <= s and s - 2 < n_units - 2:
                 finish(s - 2)
             if s >= 1:
                 quantise_h(s - 1)
                 layer2(s - 1)
-            if s + 3 < UNITS:
+            if s + 3 < n_units:
                 transposes(s + 3)
-            if s >= UNITS - 1:
+            if s >= n_units - 1:
                 finish(s - 1)
-            if s >= 1 and s % 2 == 1 and (s + 3) // 2 < E:
-                regroup_w((s + 3) // 2)
-            if s >= 2 and s % 2 == 0 and (s + 2) // 2 < E:
-                quantise_w((s + 2) // 2)
+            for e in wr_at.get(s, []):
+                regroup_w(e)
+            for e in qw_at.get(s, []):
+                quantise_w(e)

@@ -21,7 +21,7 @@ FLOPS = 2 * B * E * H * (H + D)
 PIN = False
 FIRST = [256,256,512]
 LAST = [512,256,256]
-ACT_WR = [3,5]
+ACT_WR = []
 W_LEAD = 1
 
 

@@ -18,7 +18,7 @@ TOK = 512
 WCOLS = H + D
 FLOPS = 2 * B * E * H * (H + D)
 
-PIN = False
+PIN = True
 FIRST = [256,256,512]
 LAST = [512,256,256]
 ACT_WR = []
@@ -42,7 +42,7 @@ def tile_environvectorfield_pb_t_kernel(tc, h2, W3, b3, W4, b4, out):
 
     w4_v = W4.rearrange("e (t p) d -> e p t d", t=PACK, p=P)
     b3_v = b3.rearrange("e (m p) -> (e m) p", p=P)
-    b4_v = b4.rearrange("e d -> (e d)").partition_broadcast(P)
+    b4_v = b4.rearrange("e d -> (e d)").unsqueeze(0)
     out_v = out.rearrange("(b e) d -> e b d", e=E)
 
     with ExitStack() as ctx:
@@ -64,6 +64,12 @@ def tile_environvectorfield_pb_t_kernel(tc, h2, W3, b3, W4, b4, out):
         warm_out = keep.tile([P, 1], F32, name="warm_out")
         nc.scalar.activation(out=warm_out[:], in_=warm[:], func=SILU)
 
+        b4_row = keep.tile([P, E * D], BF16, name="b4_row")
+        nc.vector.memset(b4_row[:], 0.0)
+        nc.sync.dma_start(out=b4_row[0:1, :], in_=b4_v)
+        ones = keep.tile([P, P], BF16, name="ones")
+        nc.vector.memset(ones[:], 1.0)
+
         x_raw = {}
         w_raw = {}
 
@@ -76,28 +82,30 @@ def tile_environvectorfield_pb_t_kernel(tc, h2, W3, b3, W4, b4, out):
             )
             x_raw[u] = t
 
-        def load_w(e):
+        def load_w3(e):
             t = keep.tile([P, PACK, WCOLS], BF16, name="w_raw%d" % e)
             for half in range(2):
                 nc.sync.dma_start(
                     out=t[:, 2 * half : 2 * half + 2, 0:H],
                     in_=W3[e, 256 * half : 256 * half + 256, :].rearrange("(q r) n -> q r n", r=2),
                 )
-            nc.sync.dma_start(out=t[:, :, H:WCOLS], in_=w4_v[e])
             w_raw[e] = t
 
-        b4_all = keep.tile([P, E * D], BF16, name="b4_all")
+        def load_w4(e):
+            nc.sync.dma_start(out=w_raw[e][:, :, H:WCOLS], in_=w4_v[e])
 
         w_at = {}
-        for e in range(E):
+        for e in range(1, E):
             at = max(0, first_unit[e] - W_LEAD)
             w_at[at] = w_at.get(at, []) + [e]
+        load_w3(0)
         for u in range(n_units):
             load_x(u)
+            if u == 0:
+                load_w4(0)
             for e in w_at.get(u, []):
-                load_w(e)
-            if u == 3:
-                nc.sync.dma_start(out=b4_all[:], in_=b4_v)
+                load_w3(e)
+                load_w4(e)
 
         b3_f = keep.tile([P, P], F32, name="b3_f")
         nc.vector.tensor_copy(out=b3_f[:], in_=b3_rows[:])
@@ -105,6 +113,12 @@ def tile_environvectorfield_pb_t_kernel(tc, h2, W3, b3, W4, b4, out):
         nc.tensor.transpose(b3_ps[:, 0, :], b3_f[:], ident[:])
         b3_t = keep.tile([P, E * PACK], F32, name="b3_t")
         nc.vector.tensor_copy(out=b3_t[:], in_=b3_ps[:, 0, 0 : E * PACK])
+
+        b4_all = keep.tile([P, E * D], F32, name="b4_all")
+        for j in range(E * D // TOK):
+            b4_ps = ps_z.tile([P, TOK], F32, name="z", tag="z")
+            nc.tensor.matmul(out=b4_ps[:], lhsT=ones[:], rhs=b4_row[:, TOK * j : TOK * j + TOK], start=True, stop=True)
+            nc.scalar.copy(out=b4_all[:, TOK * j : TOK * j + TOK], in_=b4_ps[:])
 
         tp = {}
         xg = {}
@@ -152,18 +166,26 @@ def tile_environvectorfield_pb_t_kernel(tc, h2, W3, b3, W4, b4, out):
             n = units[u][2]
             xq[u] = quantise(xg[u][:, 0 : PACK * n], n, TOK, "xq", 3, ring)
 
-        def regroup_w(e):
+        def regroup_w3(e):
             g = ring.tile([P, PACK * WCOLS], BF16, name="wg", tag="wg", bufs=2, align_bytes=64)
-            dst = g[:].rearrange("p (c i t) -> p c t i", i=4, t=PACK)
-            src = w_raw[e][:].rearrange("p t (c i) -> p c t i", i=4)
+            nc.vector.tensor_copy(
+                out=g[:, 0 : PACK * H].rearrange("p (c i t) -> p c t i", i=4, t=PACK),
+                in_=w_raw[e][:, :, 0:H].rearrange("p t (c i) -> p c t i", i=4),
+            )
+            wg[e] = g
+
+        def regroup_w4(e):
+            dst = wg[e][:, PACK * H : PACK * WCOLS].rearrange("p (c i t) -> p c t i", i=4, t=PACK)
+            src = w_raw[e][:, :, H:WCOLS].rearrange("p t (c i) -> p c t i", i=4)
             if e in ACT_WR:
                 nc.scalar.copy(out=dst, in_=src)
             else:
                 nc.vector.tensor_copy(out=dst, in_=src)
-            wg[e] = g
 
-        def quantise_w(e):
+        def quantise_w3(e):
             wq[e] = quantise(wg[e][:, 0 : PACK * H], H, H, "wq%d" % e, 1, keep)
+
+        def quantise_w4(e):
             w4q[e] = quantise(wg[e][:, PACK * H : PACK * WCOLS], D, D, "w4q%d" % e, 1, keep)
 
         def layer1(u, m):
@@ -243,23 +265,21 @@ def tile_environvectorfield_pb_t_kernel(tc, h2, W3, b3, W4, b4, out):
         qw_at = {}
         for e in range(1, E):
             use = first_unit[e] - 1
-            wr_at[max(-1, use - W_LEAD - 1)] = wr_at.get(max(-1, use - W_LEAD - 1), []) + [e]
-            qw_at[max(-1, use - W_LEAD)] = qw_at.get(max(-1, use - W_LEAD), []) + [e]
+            wr_at[max(0, use - W_LEAD - 1)] = wr_at.get(max(0, use - W_LEAD - 1), []) + [e]
+            qw_at[max(0, use - W_LEAD)] = qw_at.get(max(0, use - W_LEAD), []) + [e]
 
+        regroup_w3(0)
         transposes(0)
         evacuate(0)
-        regroup_w(0)
+        quantise_w3(0)
         quantise_x(0)
-        quantise_w(0)
         transposes(1)
         for m in range(PACK):
             layer1(0, m)
         evacuate(1)
+        regroup_w4(0)
+        quantise_w4(0)
         transposes(2)
-        for e in wr_at.get(-1, []):
-            regroup_w(e)
-        for e in qw_at.get(-1, []):
-            quantise_w(e)
 
         for s in range(n_units + 1):
             if s + 1 < n_units:
@@ -283,6 +303,8 @@ def tile_environvectorfield_pb_t_kernel(tc, h2, W3, b3, W4, b4, out):
             if s >= n_units - 1:
                 finish(s - 1)
             for e in wr_at.get(s, []):
-                regroup_w(e)
+                regroup_w3(e)
+                regroup_w4(e)
             for e in qw_at.get(s, []):
-                quantise_w(e)
+                quantise_w3(e)
+                quantise_w4(e)

@@ -21,8 +21,8 @@ FLOPS = 2 * B * E * H * (H + D)
 PIN = True
 FIRST = [256,256,512]
 LAST = [512,256,256]
-ACT_WR = []
-W_LEAD = 1
+ACT_WR = [0,1,2,3,4,5,6,7]
+W_LEAD = 2
 
 
 def tile_environvectorfield_pb_t_kernel(tc, h2, W3, b3, W4, b4, out):
@@ -96,12 +96,12 @@ def tile_environvectorfield_pb_t_kernel(tc, h2, W3, b3, W4, b4, out):
 
         w_at = {}
         for e in range(1, E):
-            at = max(0, first_unit[e] - W_LEAD)
+            at = max(2, first_unit[e] - W_LEAD)
             w_at[at] = w_at.get(at, []) + [e]
         load_w3(0)
         for u in range(n_units):
             load_x(u)
-            if u == 0:
+            if u == 1:
                 load_w4(0)
             for e in w_at.get(u, []):
                 load_w3(e)
@@ -166,13 +166,14 @@ def tile_environvectorfield_pb_t_kernel(tc, h2, W3, b3, W4, b4, out):
             n = units[u][2]
             xq[u] = quantise(xg[u][:, 0 : PACK * n], n, TOK, "xq", 3, ring)
 
+        def alloc_wg(e):
+            wg[e] = ring.tile([P, PACK * WCOLS], BF16, name="wg", tag="wg", bufs=2, align_bytes=64)
+
         def regroup_w3(e):
-            g = ring.tile([P, PACK * WCOLS], BF16, name="wg", tag="wg", bufs=2, align_bytes=64)
             nc.vector.tensor_copy(
-                out=g[:, 0 : PACK * H].rearrange("p (c i t) -> p c t i", i=4, t=PACK),
+                out=wg[e][:, 0 : PACK * H].rearrange("p (c i t) -> p c t i", i=4, t=PACK),
                 in_=w_raw[e][:, :, 0:H].rearrange("p t (c i) -> p c t i", i=4),
             )
-            wg[e] = g
 
         def regroup_w4(e):
             dst = wg[e][:, PACK * H : PACK * WCOLS].rearrange("p (c i t) -> p c t i", i=4, t=PACK)
@@ -268,6 +269,7 @@ def tile_environvectorfield_pb_t_kernel(tc, h2, W3, b3, W4, b4, out):
             wr_at[max(0, use - W_LEAD - 1)] = wr_at.get(max(0, use - W_LEAD - 1), []) + [e]
             qw_at[max(0, use - W_LEAD)] = qw_at.get(max(0, use - W_LEAD), []) + [e]
 
+        alloc_wg(0)
         regroup_w3(0)
         transposes(0)
         evacuate(0)
@@ -278,12 +280,15 @@ def tile_environvectorfield_pb_t_kernel(tc, h2, W3, b3, W4, b4, out):
             layer1(0, m)
         evacuate(1)
         regroup_w4(0)
-        quantise_w4(0)
         transposes(2)
 
-        for s in range(n_units + 1):
+        for s in range(n_units + 2):
+            if 1 <= s <= n_units:
+                regroup_h(s - 1)
             if s + 1 < n_units:
                 quantise_x(s + 1)
+            if s == 0:
+                quantise_w4(0)
             if s < n_units:
                 for m in range(PACK):
                     swish(s, m)
@@ -291,20 +296,18 @@ def tile_environvectorfield_pb_t_kernel(tc, h2, W3, b3, W4, b4, out):
                         layer1(s + 1, m)
             if s + 2 < n_units:
                 evacuate(s + 2)
-            if s >= 1:
-                regroup_h(s - 1)
-            if 2 <= s and s - 2 < n_units - 2:
+            for e in wr_at.get(s, []):
+                alloc_wg(e)
+                regroup_w4(e)
+            if 2 <= s:
                 finish(s - 2)
-            if s >= 1:
+            if 1 <= s <= n_units:
                 quantise_h(s - 1)
                 layer2(s - 1)
             if s + 3 < n_units:
                 transposes(s + 3)
-            if s >= n_units - 1:
-                finish(s - 1)
             for e in wr_at.get(s, []):
                 regroup_w3(e)
-                regroup_w4(e)
             for e in qw_at.get(s, []):
                 quantise_w3(e)
                 quantise_w4(e)

@@ -15,6 +15,7 @@ B, E, D, H = 1024, 8, 128, 512
 P = 128
 PACK = 4
 TOK = 512
+RUN = 8
 WCOLS = H + D
 FLOPS = 2 * B * E * H * (H + D)
 
@@ -171,13 +172,13 @@ def tile_environvectorfield_pb_t_kernel(tc, h2, W3, b3, W4, b4, out):
 
         def regroup_w3(e):
             nc.vector.tensor_copy(
-                out=wg[e][:, 0 : PACK * H].rearrange("p (c i t) -> p c t i", i=4, t=PACK),
-                in_=w_raw[e][:, :, 0:H].rearrange("p t (c i) -> p c t i", i=4),
+                out=wg[e][:, 0 : PACK * H].rearrange("p (c i t) -> p c t i", i=RUN, t=PACK),
+                in_=w_raw[e][:, :, 0:H].rearrange("p t (c i) -> p c t i", i=RUN),
             )
 
         def regroup_w4(e):
-            dst = wg[e][:, PACK * H : PACK * WCOLS].rearrange("p (c i t) -> p c t i", i=4, t=PACK)
-            src = w_raw[e][:, :, H:WCOLS].rearrange("p t (c i) -> p c t i", i=4)
+            dst = wg[e][:, PACK * H : PACK * WCOLS].rearrange("p (c i t) -> p c t i", i=RUN, t=PACK)
+            src = w_raw[e][:, :, H:WCOLS].rearrange("p t (c i) -> p c t i", i=RUN)
             if e in ACT_WR:
                 nc.scalar.copy(out=dst, in_=src)
             else:
@@ -222,8 +223,8 @@ def tile_environvectorfield_pb_t_kernel(tc, h2, W3, b3, W4, b4, out):
             n = units[u][2]
             g = ring.tile([P, PACK * TOK], BF16, name="hg", tag="hg", bufs=2, align_bytes=64)
             nc.vector.tensor_copy(
-                out=g[:, 0 : PACK * n].rearrange("p (c i t) -> p c t i", i=4, t=PACK),
-                in_=hr[u][:, :, 0:n].rearrange("p t (c i) -> p c t i", i=4),
+                out=g[:, 0 : PACK * n].rearrange("p (c i t) -> p c t i", i=RUN, t=PACK),
+                in_=hr[u][:, :, 0:n].rearrange("p t (c i) -> p c t i", i=RUN),
             )
             hg[u] = g
 

@@ -22,7 +22,11 @@ FLOPS = 2 * B * E * H * (H + D)
 PIN = True
 FIRST = [256,256,512]
 LAST = [512,256,256]
-ACT_WR = [0,1,2,3,4,5,6,7]
+W4_LATE = 0
+PE_COLS = 128
+PE_FROM = 5
+LATE_F = 3
+AHEAD = 0
 W_LEAD = 2
 
 
@@ -51,12 +55,15 @@ def tile_environvectorfield_pb_t_kernel(tc, h2, W3, b3, W4, b4, out):
         ring = ctx.enter_context(tc.tile_pool(name="ring", bufs=2))
         ps_t = ctx.enter_context(tc.psum_pool(name="ps_t", bufs=2))
         ps_z = ctx.enter_context(tc.psum_pool(name="ps_z", bufs=4))
-        ps_o = ctx.enter_context(tc.psum_pool(name="ps_o", bufs=2))
+        ps_o = ctx.enter_context(tc.psum_pool(name="ps_o", bufs=1))
+        ps_w = ctx.enter_context(tc.psum_pool(name="ps_w", bufs=1))
         if PIN:
             ctx.enter_context(tc.manual_schedule())
 
         ident = keep.tile([P, P], F32, name="ident")
         make_identity(nc, ident[:])
+        ident_b = keep.tile([P, P], BF16, name="ident_b")
+        make_identity(nc, ident_b[:])
         b3_rows = keep.tile([P, P], BF16, name="b3_rows")
         nc.vector.memset(b3_rows[:], 0.0)
         nc.sync.dma_start(out=b3_rows[0 : E * PACK, :], in_=b3_v)
@@ -67,12 +74,12 @@ def tile_environvectorfield_pb_t_kernel(tc, h2, W3, b3, W4, b4, out):
 
         b4_row = keep.tile([P, E * D], BF16, name="b4_row")
         nc.vector.memset(b4_row[:], 0.0)
-        nc.sync.dma_start(out=b4_row[0:1, :], in_=b4_v)
         ones = keep.tile([P, P], BF16, name="ones")
         nc.vector.memset(ones[:], 1.0)
 
         x_raw = {}
-        w_raw = {}
+        w3_raw = {}
+        w4_raw = {}
 
         def load_x(u):
             e, t0, n = units[u]
@@ -84,29 +91,42 @@ def tile_environvectorfield_pb_t_kernel(tc, h2, W3, b3, W4, b4, out):
             x_raw[u] = t
 
         def load_w3(e):
-            t = keep.tile([P, PACK, WCOLS], BF16, name="w_raw%d" % e)
-            for half in range(2):
-                nc.sync.dma_start(
-                    out=t[:, 2 * half : 2 * half + 2, 0:H],
-                    in_=W3[e, 256 * half : 256 * half + 256, :].rearrange("(q r) n -> q r n", r=2),
-                )
-            w_raw[e] = t
+            t = keep.tile([P, PACK, H], BF16, name="w3_raw%d" % e)
+            nc.sync.dma_start(
+                out=t[:].rearrange("p (u r) n -> p u (r n)", u=2),
+                in_=W3[e].rearrange("(u q r) n -> q u (r n)", u=2, r=2),
+            )
+            w3_raw[e] = t
 
         def load_w4(e):
-            nc.sync.dma_start(out=w_raw[e][:, :, H:WCOLS], in_=w4_v[e])
+            t = keep.tile([P, PACK, D], BF16, name="w4_raw%d" % e)
+            nc.sync.dma_start(out=t[:], in_=w4_v[e])
+            w4_raw[e] = t
 
         w_at = {}
         for e in range(1, E):
             at = max(2, first_unit[e] - W_LEAD)
             w_at[at] = w_at.get(at, []) + [e]
-        load_w3(0)
-        for u in range(n_units):
+        load_x(0)
+        nc.sync.dma_start(out=b4_row[0:1, :], in_=b4_v)
+        t = keep.tile([P, PACK, H], BF16, name="w3_raw0")
+        for c0 in (0, H // 2):
+            for q in range(2):
+                nc.sync.dma_start(
+                    out=t[:, 2 * q : 2 * q + 2, c0 : c0 + H // 2],
+                    in_=W3[0, 256 * q : 256 * q + 256, c0 : c0 + H // 2].rearrange("(q r) n -> q r n", r=2),
+                )
+        w3_raw[0] = t
+        load_x(1)
+        load_w3(1)
+        load_x(2)
+        load_w4(0)
+        for u in range(3, n_units):
             load_x(u)
-            if u == 1:
-                load_w4(0)
             for e in w_at.get(u, []):
                 load_w3(e)
-                load_w4(e)
+                load_w4(e - 1)
+        load_w4(E - 1)
 
         b3_f = keep.tile([P, P], F32, name="b3_f")
         nc.vector.tensor_copy(out=b3_f[:], in_=b3_rows[:])
@@ -115,19 +135,24 @@ def tile_environvectorfield_pb_t_kernel(tc, h2, W3, b3, W4, b4, out):
         b3_t = keep.tile([P, E * PACK], F32, name="b3_t")
         nc.vector.tensor_copy(out=b3_t[:], in_=b3_ps[:, 0, 0 : E * PACK])
 
-        b4_all = keep.tile([P, E * D], F32, name="b4_all")
-        for j in range(E * D // TOK):
-            b4_ps = ps_z.tile([P, TOK], F32, name="z", tag="z")
-            nc.tensor.matmul(out=b4_ps[:], lhsT=ones[:], rhs=b4_row[:, TOK * j : TOK * j + TOK], start=True, stop=True)
-            nc.scalar.copy(out=b4_all[:, TOK * j : TOK * j + TOK], in_=b4_ps[:])
+        b4_all = keep.tile([P, E * D], BF16, name="b4_all")
+
+        def spread_b4():
+            bank = ps_w.tile([P, 2 * TOK], BF16, name="w", tag="w")
+            for j in range(E * D // TOK):
+                cols = slice(TOK * j, TOK * j + TOK)
+                nc.tensor.matmul(out=bank[:, cols], lhsT=ones[:], rhs=b4_row[:, cols], start=True, stop=True)
+            nc.scalar.copy(out=b4_all[:], in_=bank[:])
 
         tp = {}
         xg = {}
         xq = {}
         wg = {}
+        w4g = {}
         wq = {}
         w4q = {}
         zt = {}
+        zb = {}
         hr = {}
         hg = {}
         hq = {}
@@ -168,35 +193,68 @@ def tile_environvectorfield_pb_t_kernel(tc, h2, W3, b3, W4, b4, out):
             xq[u] = quantise(xg[u][:, 0 : PACK * n], n, TOK, "xq", 3, ring)
 
         def alloc_wg(e):
-            wg[e] = ring.tile([P, PACK * WCOLS], BF16, name="wg", tag="wg", bufs=2, align_bytes=64)
+            wg[e] = ring.tile([P, PACK * H], BF16, name="wg", tag="wg", bufs=2, align_bytes=64)
 
-        def regroup_w3(e):
-            nc.vector.tensor_copy(
-                out=wg[e][:, 0 : PACK * H].rearrange("p (c i t) -> p c t i", i=RUN, t=PACK),
-                in_=w_raw[e][:, :, 0:H].rearrange("p t (c i) -> p c t i", i=RUN),
-            )
-
-        def regroup_w4(e):
-            dst = wg[e][:, PACK * H : PACK * WCOLS].rearrange("p (c i t) -> p c t i", i=RUN, t=PACK)
-            src = w_raw[e][:, :, H:WCOLS].rearrange("p t (c i) -> p c t i", i=RUN)
-            if e in ACT_WR:
+        def regroup_w3(e, c0=0, c1=H, engine="vector"):
+            dst = wg[e][:, PACK * c0 : PACK * c1].rearrange("p (c i t) -> p c t i", i=RUN, t=PACK)
+            src = w3_raw[e][:, :, c0:c1].rearrange("p t (c i) -> p c t i", i=RUN)
+            if engine == "scalar":
                 nc.scalar.copy(out=dst, in_=src)
             else:
                 nc.vector.tensor_copy(out=dst, in_=src)
 
-        def quantise_w3(e):
-            wq[e] = quantise(wg[e][:, 0 : PACK * H], H, H, "wq%d" % e, 1, keep)
+        def regroup_w4(e):
+            w4g[e] = ring.tile([P, PACK * D], BF16, name="w4g", tag="w4g", bufs=2, align_bytes=64)
+            dst = w4g[e][:].rearrange("p (c i t) -> p c t i", i=RUN, t=PACK)
+            src = w4_raw[e][:].rearrange("p t (c i) -> p c t i", i=RUN)
+            nc.vector.tensor_copy(out=dst, in_=src)
+
+        pe_bank = {}
+
+        def interleave(key, raw, c0, c1):
+            bank = ps_w.tile([P, 2 * TOK], BF16, name="w", tag="w")
+            for j in range((c1 - c0) // P):
+                nc.tensor.matmul(
+                    out=bank[:, TOK * j : TOK * j + TOK].rearrange("p (c i t) -> p c t i", i=RUN, t=PACK),
+                    lhsT=ident_b[:],
+                    rhs=raw[:, :, c0 + P * j : c0 + P * j + P].rearrange("p t (c i) -> p c t i", i=RUN),
+                    start=True,
+                    stop=True,
+                )
+            pe_bank[key] = bank
+
+        def empty_w4(e):
+            w4g[e] = ring.tile([P, PACK * D], BF16, name="w4g", tag="w4g", bufs=2, align_bytes=64)
+            nc.scalar.copy(out=w4g[e][:], in_=pe_bank[("w4", e)][:, 0 : PACK * D])
+
+        def empty_w3(e):
+            c0 = H - PE_COLS
+            nc.scalar.copy(out=wg[e][:, PACK * c0 :], in_=pe_bank[("w3", e)][:, 0 : PACK * PE_COLS])
+
+        def quantise_w3(e, c0=0, c1=H):
+            if e not in wq:
+                wq[e] = (
+                    keep.tile([P, H], U32, name="wqc%d" % e, align_bytes=64),
+                    keep.tile([P, H], U8, name="wqs%d" % e, align_bytes=64),
+                )
+            codes, scales = wq[e]
+            nc.vector.quantize_mx(
+                out=codes[:, c0:c1].bitcast(FP8X4), scales=scales[:, c0:c1], in_=wg[e][:, PACK * c0 : PACK * c1]
+            )
 
         def quantise_w4(e):
-            w4q[e] = quantise(wg[e][:, PACK * H : PACK * WCOLS], D, D, "w4q%d" % e, 1, keep)
+            w4q[e] = quantise(w4g[e][:], D, D, "w4q%d" % e, 1, keep)
 
         def layer1(u, m):
             e, t0, n = units[u]
-            z = ps_z.tile([P, TOK], F32, name="z", tag="z")
+            share = TOK // n
+            if m % share == 0:
+                zb[u] = ps_z.tile([P, TOK], F32, name="z", tag="z")
+            z = zb[u][:, n * (m % share) : n * (m % share) + n]
             wc, ws = wq[e]
             xc, xs = xq[u]
             nc.tensor.matmul_mx(
-                out=z[:, 0:n],
+                out=z,
                 lhsT=wc[:, P * m : P * m + P].bitcast(FP8X4),
                 lhsT_scale=ws[:, P * m : P * m + P],
                 rhs=xc[:, 0:n].bitcast(FP8X4),
@@ -213,7 +271,7 @@ def tile_environvectorfield_pb_t_kernel(tc, h2, W3, b3, W4, b4, out):
             col = PACK * e + m
             nc.scalar.activation(
                 out=hr[u][:, m, 0:n],
-                in_=zt[(u, m)][:, 0:n],
+                in_=zt[(u, m)],
                 func=SILU,
                 bias=b3_t[:, col : col + 1],
                 scale=1.0,
@@ -234,7 +292,10 @@ def tile_environvectorfield_pb_t_kernel(tc, h2, W3, b3, W4, b4, out):
 
         def layer2(u):
             e, t0, n = units[u]
-            o = ps_o.tile([P, TOK // P, D], F32, name="o", tag="o")
+            if u >= n_units - LATE_F and u % 2:
+                o = ps_w.tile([P, TOK // P, D], F32, name="w", tag="w")
+            else:
+                o = ps_o.tile([P, TOK // P, D], F32, name="o", tag="o")
             hc, hs = hq[u]
             wc, ws = w4q[e]
             for c in range(n // P):
@@ -265,50 +326,98 @@ def tile_environvectorfield_pb_t_kernel(tc, h2, W3, b3, W4, b4, out):
 
         wr_at = {}
         qw_at = {}
+        w4_at = {}
+        q4_at = {}
         for e in range(1, E):
             use = first_unit[e] - 1
-            wr_at[max(0, use - W_LEAD - 1)] = wr_at.get(max(0, use - W_LEAD - 1), []) + [e]
-            qw_at[max(0, use - W_LEAD)] = qw_at.get(max(0, use - W_LEAD), []) + [e]
+            if e > 1:
+                wr_at.setdefault(max(1, use - W_LEAD - 1), []).append(e)
+            qw_at.setdefault(max(1, use - W_LEAD), []).append(e)
+            w4_at.setdefault(use + W4_LATE, []).append(e)
+            q4_at.setdefault(use + W4_LATE + 1, []).append(e)
+
+        pe3_at = {}
+        for e in range(PE_FROM, E):
+            if PE_COLS:
+                pe3_at.setdefault(first_unit[e] - 1 - W_LEAD - 1, []).append(e)
 
         alloc_wg(0)
-        regroup_w3(0)
         transposes(0)
         evacuate(0)
-        quantise_w3(0)
+        spread_b4()
+        regroup_w3(0, 0, 256)
+        quantise_w3(0, 0, 256)
         quantise_x(0)
+        layer1(0, 0)
+        layer1(0, 1)
+        regroup_w3(0, 256, 512)
         transposes(1)
-        for m in range(PACK):
-            layer1(0, m)
+        swish(0, 0)
+        swish(0, 1)
         evacuate(1)
-        regroup_w4(0)
+        quantise_w3(0, 256, 512)
+        layer1(0, 2)
+        layer1(0, 3)
         transposes(2)
+        quantise_x(1)
+        for m in range(PACK):
+            layer1(1, m)
+            if m < 2:
+                swish(0, m + 2)
+        evacuate(2)
+        alloc_wg(1)
+        regroup_w3(1)
+        transposes(3)
 
-        for s in range(n_units + 2):
-            if 1 <= s <= n_units:
+        ev_at = {}
+        qx_at = {}
+        for u in range(3, n_units):
+            ev_at.setdefault(u - 3 if u >= n_units - AHEAD else u - 2, []).append(u)
+        for u in range(2, n_units):
+            qx_at.setdefault(u - 2 if u >= n_units - AHEAD else u - 1, []).append(u)
+        fin_at = {}
+        for u in range(n_units):
+            fin_at.setdefault(u + 3 if u >= n_units - LATE_F else u + 2, []).append(u)
+
+        for s in range(1, n_units + 3):
+            if s <= n_units:
                 regroup_h(s - 1)
-            if s + 1 < n_units:
-                quantise_x(s + 1)
-            if s == 0:
-                quantise_w4(0)
+            for u in qx_at.get(s, []):
+                quantise_x(u)
             if s < n_units:
                 for m in range(PACK):
                     swish(s, m)
                     if s + 1 < n_units:
                         layer1(s + 1, m)
-            if s + 2 < n_units:
-                evacuate(s + 2)
-            for e in wr_at.get(s, []):
-                alloc_wg(e)
-                regroup_w4(e)
-            if 2 <= s:
-                finish(s - 2)
-            if 1 <= s <= n_units:
+            if s == 1:
+                regroup_w4(0)
+            for u in ev_at.get(s, []):
+                evacuate(u)
+            for e in w4_at.get(s, []):
+                empty_w4(e)
+            for e in pe3_at.get(s, []):
+                empty_w3(e)
+            if s == 1:
+                quantise_w4(0)
+            for u in fin_at.get(s, []):
+                finish(u)
+            if s <= n_units:
                 quantise_h(s - 1)
                 layer2(s - 1)
-            if s + 3 < n_units:
-                transposes(s + 3)
+            for u in ev_at.get(s + 1, []):
+                transposes(u)
             for e in wr_at.get(s, []):
-                regroup_w3(e)
+                if e < PE_FROM:
+                    alloc_wg(e)
+                    regroup_w3(e)
+                else:
+                    regroup_w3(e, 0, H - PE_COLS)
+            for e in w4_at.get(s + 1, []):
+                interleave(("w4", e), w4_raw[e], 0, D)
+            for e in pe3_at.get(s + 1, []):
+                alloc_wg(e)
+                interleave(("w3", e), w3_raw[e], H - PE_COLS, H)
             for e in qw_at.get(s, []):
                 quantise_w3(e)
+            for e in q4_at.get(s, []):
                 quantise_w4(e)

@@ -26,7 +26,8 @@ W4_LATE = 0
 PE_COLS = 128
 PE_FROM = 5
 LATE_F = 3
-AHEAD = 0
+SHARE_H = 2
+AHEAD = 1
 W_LEAD = 2
 
 
@@ -108,7 +109,6 @@ def tile_environvectorfield_pb_t_kernel(tc, h2, W3, b3, W4, b4, out):
             at = max(2, first_unit[e] - W_LEAD)
             w_at[at] = w_at.get(at, []) + [e]
         load_x(0)
-        nc.sync.dma_start(out=b4_row[0:1, :], in_=b4_v)
         t = keep.tile([P, PACK, H], BF16, name="w3_raw0")
         for c0 in (0, H // 2):
             for q in range(2):
@@ -116,6 +116,8 @@ def tile_environvectorfield_pb_t_kernel(tc, h2, W3, b3, W4, b4, out):
                     out=t[:, 2 * q : 2 * q + 2, c0 : c0 + H // 2],
                     in_=W3[0, 256 * q : 256 * q + 256, c0 : c0 + H // 2].rearrange("(q r) n -> q r n", r=2),
                 )
+            if c0 == 0:
+                nc.sync.dma_start(out=b4_row[0:1, :], in_=b4_v)
         w3_raw[0] = t
         load_x(1)
         load_w3(1)
@@ -279,12 +281,16 @@ def tile_environvectorfield_pb_t_kernel(tc, h2, W3, b3, W4, b4, out):
 
         def regroup_h(u):
             n = units[u][2]
-            g = ring.tile([P, PACK * TOK], BF16, name="hg", tag="hg", bufs=2, align_bytes=64)
-            nc.vector.tensor_copy(
-                out=g[:, 0 : PACK * n].rearrange("p (c i t) -> p c t i", i=RUN, t=PACK),
-                in_=hr[u][:, :, 0:n].rearrange("p t (c i) -> p c t i", i=RUN),
-            )
-            hg[u] = g
+            hg[u] = ring.tile([P, PACK * TOK], BF16, name="hg", tag="hg", bufs=2, align_bytes=64)
+            cut = n - (P if u >= n_units - SHARE_H else 0)
+            for engine, c0, c1 in (("vector", 0, cut), ("scalar", cut, n)):
+                if c0 < c1:
+                    dst = hg[u][:, PACK * c0 : PACK * c1].rearrange("p (c i t) -> p c t i", i=RUN, t=PACK)
+                    src = hr[u][:, :, c0:c1].rearrange("p t (c i) -> p c t i", i=RUN)
+                    if engine == "scalar":
+                        nc.scalar.copy(out=dst, in_=src)
+                    else:
+                        nc.vector.tensor_copy(out=dst, in_=src)
 
         def quantise_h(u):
             n = units[u][2]

@@ -26,6 +26,7 @@ W4_LATE = 0
 PE_COLS = 128
 PE_FROM = 5
 LATE_F = 3
+WARM = 6
 SHARE_H = 2
 AHEAD = 1
 W_LEAD = 2
@@ -73,10 +74,10 @@ def tile_environvectorfield_pb_t_kernel(tc, h2, W3, b3, W4, b4, out):
         warm_out = keep.tile([P, 1], F32, name="warm_out")
         nc.scalar.activation(out=warm_out[:], in_=warm[:], func=SILU)
 
+        ones = keep.tile([P, TOK], BF16, name="ones")
+        nc.vector.memset(ones[:], 1.0)
         b4_row = keep.tile([P, E * D], BF16, name="b4_row")
         nc.vector.memset(b4_row[:], 0.0)
-        ones = keep.tile([P, P], BF16, name="ones")
-        nc.vector.memset(ones[:], 1.0)
 
         x_raw = {}
         w3_raw = {}
@@ -130,6 +131,10 @@ def tile_environvectorfield_pb_t_kernel(tc, h2, W3, b3, W4, b4, out):
                 load_w4(e - 1)
         load_w4(E - 1)
 
+        idle = ps_z.tile([P, TOK], F32, name="z", tag="z")
+        for j in range(WARM):
+            nc.tensor.matmul(out=idle[:], lhsT=ones[:, 0:P], rhs=ones[:], start=True, stop=True)
+
         b3_f = keep.tile([P, P], F32, name="b3_f")
         nc.vector.tensor_copy(out=b3_f[:], in_=b3_rows[:])
         b3_ps = ps_t.tile([P, 4, P], F32, name="tp", tag="tp")
@@ -143,7 +148,7 @@ def tile_environvectorfield_pb_t_kernel(tc, h2, W3, b3, W4, b4, out):
             bank = ps_w.tile([P, 2 * TOK], BF16, name="w", tag="w")
             for j in range(E * D // TOK):
                 cols = slice(TOK * j, TOK * j + TOK)
-                nc.tensor.matmul(out=bank[:, cols], lhsT=ones[:], rhs=b4_row[:, cols], start=True, stop=True)
+                nc.tensor.matmul(out=bank[:, cols], lhsT=ones[:, 0:P], rhs=b4_row[:, cols], start=True, stop=True)
             nc.scalar.copy(out=b4_all[:], in_=bank[:])
 
         tp = {}

@@ -24,9 +24,8 @@ FIRST = [256,256,512]
 LAST = [512,256,256]
 W4_LATE = 0
 PE_COLS = 128
-PE_FROM = 5
+PE_FROM = 6
 LATE_F = 3
-WARM = 6
 SHARE_H = 2
 AHEAD = 1
 W_LEAD = 2
@@ -118,9 +117,9 @@ def tile_environvectorfield_pb_t_kernel(tc, h2, W3, b3, W4, b4, out):
                     in_=W3[0, 256 * q : 256 * q + 256, c0 : c0 + H // 2].rearrange("(q r) n -> q r n", r=2),
                 )
             if c0 == 0:
+                load_x(1)
                 nc.sync.dma_start(out=b4_row[0:1, :], in_=b4_v)
         w3_raw[0] = t
-        load_x(1)
         load_w3(1)
         load_x(2)
         load_w4(0)
@@ -132,9 +131,12 @@ def tile_environvectorfield_pb_t_kernel(tc, h2, W3, b3, W4, b4, out):
         load_w4(E - 1)
 
         idle = ps_z.tile([P, TOK], F32, name="z", tag="z")
-        for j in range(WARM):
-            nc.tensor.matmul(out=idle[:], lhsT=ones[:, 0:P], rhs=ones[:], start=True, stop=True)
 
+        def warm_up(count):
+            for j in range(count):
+                nc.tensor.matmul(out=idle[:], lhsT=ones[:, 0:P], rhs=ones[:], start=True, stop=True)
+
+        warm_up(3)
         b3_f = keep.tile([P, P], F32, name="b3_f")
         nc.vector.tensor_copy(out=b3_f[:], in_=b3_rows[:])
         b3_ps = ps_t.tile([P, 4, P], F32, name="tp", tag="tp")
@@ -325,15 +327,17 @@ def tile_environvectorfield_pb_t_kernel(tc, h2, W3, b3, W4, b4, out):
             e, t0, n = units[u]
             nch = n // P
             res = ring.tile([P, TOK // P, D], F32, name="res", tag="res", bufs=8)
-            nc.vector.tensor_tensor(
-                out=res[:, 0:nch, :],
-                in0=ot[u][:, 0:nch, :],
-                in1=b4_all[:, D * e : D * e + D].unsqueeze(1).to_broadcast([P, nch, D]),
-                op=ADD,
-            )
-            nc.sync.dma_start(
-                out=out_v[e, t0 : t0 + n, :].rearrange("(c p) d -> p c d", p=P), in_=res[:, 0:nch, :]
-            )
+            parts = [(c, c + 1) for c in range(nch)] if u == n_units - 1 else [(0, nch)]
+            for c0, c1 in parts:
+                nc.vector.tensor_tensor(
+                    out=res[:, c0:c1, :],
+                    in0=ot[u][:, c0:c1, :],
+                    in1=b4_all[:, D * e : D * e + D].unsqueeze(1).to_broadcast([P, c1 - c0, D]),
+                    op=ADD,
+                )
+                nc.sync.dma_start(
+                    out=out_v[e, t0 + P * c0 : t0 + P * c1, :].rearrange("(c p) d -> p c d", p=P), in_=res[:, c0:c1, :]
+                )
 
         wr_at = {}
         qw_at = {}
@@ -353,28 +357,31 @@ def tile_environvectorfield_pb_t_kernel(tc, h2, W3, b3, W4, b4, out):
                 pe3_at.setdefault(first_unit[e] - 1 - W_LEAD - 1, []).append(e)
 
         alloc_wg(0)
+        warm_up(2)
         transposes(0)
         evacuate(0)
-        spread_b4()
         regroup_w3(0, 0, 256)
         quantise_w3(0, 0, 256)
         quantise_x(0)
+        transposes(1)
+        evacuate(1)
+        spread_b4()
         layer1(0, 0)
         layer1(0, 1)
         regroup_w3(0, 256, 512)
-        transposes(1)
         swish(0, 0)
         swish(0, 1)
-        evacuate(1)
         quantise_w3(0, 256, 512)
+        quantise_x(1)
         layer1(0, 2)
         layer1(0, 3)
-        transposes(2)
-        quantise_x(1)
         for m in range(PACK):
             layer1(1, m)
             if m < 2:
                 swish(0, m + 2)
+        transposes(2)
+        swish(1, 0)
+        swish(1, 1)
         evacuate(2)
         alloc_wg(1)
         regroup_w3(1)
@@ -393,27 +400,29 @@ def tile_environvectorfield_pb_t_kernel(tc, h2, W3, b3, W4, b4, out):
         for s in range(1, n_units + 3):
             if s <= n_units:
                 regroup_h(s - 1)
+            if s == 1:
+                regroup_w4(0)
+                quantise_h(0)
+                quantise_w4(0)
             for u in qx_at.get(s, []):
                 quantise_x(u)
             if s < n_units:
                 for m in range(PACK):
-                    swish(s, m)
+                    if s > 1 or m > 1:
+                        swish(s, m)
                     if s + 1 < n_units:
                         layer1(s + 1, m)
-            if s == 1:
-                regroup_w4(0)
             for u in ev_at.get(s, []):
                 evacuate(u)
             for e in w4_at.get(s, []):
                 empty_w4(e)
             for e in pe3_at.get(s, []):
                 empty_w3(e)
-            if s == 1:
-                quantise_w4(0)
             for u in fin_at.get(s, []):
                 finish(u)
             if s <= n_units:
-                quantise_h(s - 1)
+                if s > 1:
+                    quantise_h(s - 1)
                 layer2(s - 1)
             for u in ev_at.get(s + 1, []):
                 transposes(u)

@@ -67,7 +67,6 @@ def tile_environvectorfield_pb_t_kernel(tc, h2, W3, b3, W4, b4, out):
         make_identity(nc, ident_b[:])
         b3_rows = keep.tile([P, P], BF16, name="b3_rows")
         nc.vector.memset(b3_rows[:], 0.0)
-        nc.sync.dma_start(out=b3_rows[0 : E * PACK, :], in_=b3_v)
         warm = keep.tile([P, 1], F32, name="warm")
         nc.vector.memset(warm[:], 0.0)
         warm_out = keep.tile([P, 1], F32, name="warm_out")
@@ -109,17 +108,10 @@ def tile_environvectorfield_pb_t_kernel(tc, h2, W3, b3, W4, b4, out):
             at = max(2, first_unit[e] - W_LEAD)
             w_at[at] = w_at.get(at, []) + [e]
         load_x(0)
-        t = keep.tile([P, PACK, H], BF16, name="w3_raw0")
-        for c0 in (0, H // 2):
-            for q in range(2):
-                nc.sync.dma_start(
-                    out=t[:, 2 * q : 2 * q + 2, c0 : c0 + H // 2],
-                    in_=W3[0, 256 * q : 256 * q + 256, c0 : c0 + H // 2].rearrange("(q r) n -> q r n", r=2),
-                )
-            if c0 == 0:
-                load_x(1)
-                nc.sync.dma_start(out=b4_row[0:1, :], in_=b4_v)
-        w3_raw[0] = t
+        load_w3(0)
+        nc.sync.dma_start(out=b3_rows[0 : E * PACK, :], in_=b3_v)
+        nc.sync.dma_start(out=b4_row[0:1, :], in_=b4_v)
+        load_x(1)
         load_w3(1)
         load_x(2)
         load_w4(0)
@@ -138,11 +130,7 @@ def tile_environvectorfield_pb_t_kernel(tc, h2, W3, b3, W4, b4, out):
 
         warm_up(3)
         b3_f = keep.tile([P, P], F32, name="b3_f")
-        nc.vector.tensor_copy(out=b3_f[:], in_=b3_rows[:])
-        b3_ps = ps_t.tile([P, 4, P], F32, name="tp", tag="tp")
-        nc.tensor.transpose(b3_ps[:, 0, :], b3_f[:], ident[:])
         b3_t = keep.tile([P, E * PACK], F32, name="b3_t")
-        nc.vector.tensor_copy(out=b3_t[:], in_=b3_ps[:, 0, 0 : E * PACK])
 
         b4_all = keep.tile([P, E * D], BF16, name="b4_all")
 
@@ -360,15 +348,19 @@ def tile_environvectorfield_pb_t_kernel(tc, h2, W3, b3, W4, b4, out):
         warm_up(2)
         transposes(0)
         evacuate(0)
+        spread_b4()
         regroup_w3(0, 0, 256)
+        nc.vector.tensor_copy(out=b3_f[:], in_=b3_rows[:])
+        b3_ps = ps_t.tile([P, 4, P], F32, name="tp", tag="tp")
+        nc.tensor.transpose(b3_ps[:, 0, :], b3_f[:], ident[:])
         quantise_w3(0, 0, 256)
         quantise_x(0)
         transposes(1)
         evacuate(1)
-        spread_b4()
         layer1(0, 0)
         layer1(0, 1)
         regroup_w3(0, 256, 512)
+        nc.vector.tensor_copy(out=b3_t[:], in_=b3_ps[:, 0, 0 : E * PACK])
         swish(0, 0)
         swish(0, 1)
         quantise_w3(0, 256, 512)

from contextlib import ExitStack

import concourse.mybir as mybir
from concourse.masks import make_identity

F32 = mybir.dt.float32
BF16 = mybir.dt.bfloat16
U32 = mybir.dt.uint32
U8 = mybir.dt.uint8
FP8X4 = mybir.dt.float8_e4m3fn_x4
SILU = mybir.ActivationFunctionType.Silu
ADD = mybir.AluOpType.add

B, E, D, H = 1024, 8, 128, 512
P = 128
PACK = 4
TOK = 512
RUN = 8
WCOLS = H + D
FLOPS = 2 * B * E * H * (H + D)

PIN = True
FIRST = [256,256,512]
LAST = [512,256,256]
W4_LATE = 0
PE_COLS = 128
PE_FROM = 6
LATE_F = 3
SHARE_H = 2
AHEAD = 1
W_LEAD = 2


def tile_environvectorfield_pb_t_kernel(tc, h2, W3, b3, W4, b4, out):
    nc = tc.nc
    units = []
    for e in range(E):
        sizes = FIRST if e == 0 else (LAST if e == E - 1 else [TOK, TOK])
        t0 = 0
        for n in sizes:
            units.append((e, t0, n))
            t0 += n
    n_units = len(units)
    first_unit = {}
    for u in range(n_units):
        if units[u][0] not in first_unit:
            first_unit[units[u][0]] = u

    w4_v = W4.rearrange("e (t p) d -> e p t d", t=PACK, p=P)
    b3_v = b3.rearrange("e (m p) -> (e m) p", p=P)
    b4_v = b4.rearrange("e d -> (e d)").unsqueeze(0)
    out_v = out.rearrange("(b e) d -> e b d", e=E)

    with ExitStack() as ctx:
        keep = ctx.enter_context(tc.tile_pool(name="keep", bufs=1))
        ring = ctx.enter_context(tc.tile_pool(name="ring", bufs=2))
        ps_t = ctx.enter_context(tc.psum_pool(name="ps_t", bufs=2))
        ps_z = ctx.enter_context(tc.psum_pool(name="ps_z", bufs=4))
        ps_o = ctx.enter_context(tc.psum_pool(name="ps_o", bufs=1))
        ps_w = ctx.enter_context(tc.psum_pool(name="ps_w", bufs=1))
        if PIN:
            ctx.enter_context(tc.manual_schedule())

        ident = keep.tile([P, P], F32, name="ident")
        make_identity(nc, ident[:])
        ident_b = keep.tile([P, P], BF16, name="ident_b")
        make_identity(nc, ident_b[:])
        b3_rows = keep.tile([P, P], BF16, name="b3_rows")
        nc.vector.memset(b3_rows[:], 0.0)
        warm = keep.tile([P, 1], F32, name="warm")
        nc.vector.memset(warm[:], 0.0)
        warm_out = keep.tile([P, 1], F32, name="warm_out")
        nc.scalar.activation(out=warm_out[:], in_=warm[:], func=SILU)

        ones = keep.tile([P, TOK], BF16, name="ones")
        nc.vector.memset(ones[:], 1.0)
        b4_row = keep.tile([P, E * D], BF16, name="b4_row")
        nc.vector.memset(b4_row[:], 0.0)

        x_raw = {}
        w3_raw = {}
        w4_raw = {}

        def load_x(u):
            e, t0, n = units[u]
            t = keep.tile([P, (n // P) * H], BF16, name="x_raw%d" % u)
            nc.sync.dma_start(
                out=t[:].rearrange("p (c k) -> p c k", k=H),
                in_=h2[t0 : t0 + n, e, :].rearrange("(c p) k -> p c k", p=P),
            )
            x_raw[u] = t

        def load_w3(e):
            t = keep.tile([P, PACK, H], BF16, name="w3_raw%d" % e)
            nc.sync.dma_start(
                out=t[:].rearrange("p (u r) n -> p u (r n)", u=2),
                in_=W3[e].rearrange("(u q r) n -> q u (r n)", u=2, r=2),
            )
            w3_raw[e] = t

        def load_w4(e):
            t = keep.tile([P, PACK, D], BF16, name="w4_raw%d" % e)
            nc.sync.dma_start(out=t[:], in_=w4_v[e])
            w4_raw[e] = t

        w_at = {}
        for e in range(1, E):
            at = max(2, first_unit[e] - W_LEAD)
            w_at[at] = w_at.get(at, []) + [e]
        load_x(0)
        load_w3(0)
        nc.sync.dma_start(out=b3_rows[0 : E * PACK, :], in_=b3_v)
        nc.sync.dma_start(out=b4_row[0:1, :], in_=b4_v)
        load_x(1)
        load_w3(1)
        load_x(2)
        load_w4(0)
        for u in range(3, n_units):
            load_x(u)
            for e in w_at.get(u, []):
                load_w3(e)
                load_w4(e - 1)
        load_w4(E - 1)

        idle = ps_z.tile([P, TOK], F32, name="z", tag="z")

        def warm_up(count):
            for j in range(count):
                nc.tensor.matmul(out=idle[:], lhsT=ones[:, 0:P], rhs=ones[:], start=True, stop=True)

        warm_up(3)
        b3_f = keep.tile([P, P], F32, name="b3_f")
        b3_t = keep.tile([P, E * PACK], F32, name="b3_t")

        b4_all = keep.tile([P, E * D], BF16, name="b4_all")

        def spread_b4():
            bank = ps_w.tile([P, 2 * TOK], BF16, name="w", tag="w")
            for j in range(E * D // TOK):
                cols = slice(TOK * j, TOK * j + TOK)
                nc.tensor.matmul(out=bank[:, cols], lhsT=ones[:, 0:P], rhs=b4_row[:, cols], start=True, stop=True)
            nc.scalar.copy(out=b4_all[:], in_=bank[:])

        tp = {}
        xg = {}
        xq = {}
        wg = {}
        w4g = {}
        wq = {}
        w4q = {}
        zt = {}
        zb = {}
        hr = {}
        hg = {}
        hq = {}
        ot = {}

        def transposes(u):
            n = units[u][2]
            words = x_raw[u][:].bitcast(F32)
            banks = []
            for j in range(n // 256):
                bank = ps_t.tile([P, 4, P], F32, name="tp", tag="tp")
                for s in range(4):
                    col = 256 * (2 * j + s // 2) + P * (s % 2)
                    nc.tensor.transpose(bank[:, s, :], words[:, col : col + P], ident[:])
                banks.append(bank)
            tp[u] = banks

        def evacuate(u):
            g = ring.tile([P, PACK * TOK], BF16, name="xg", tag="xg", bufs=3, align_bytes=64)
            words = g[:].bitcast(F32).rearrange("p (c b w) -> p c b w", b=P, w=2)
            for j in range(len(tp[u])):
                nc.scalar.copy(
                    out=words[:, 2 * j : 2 * j + 2],
                    in_=tp[u][j][:].rearrange("p (c w) b -> p c b w", w=2),
                )
            xg[u] = g

        def quantise(src, width, full, tag, bufs, pool):
            codes = pool.tile([P, full], U32, name=tag + "c", tag=tag + "c", bufs=bufs, align_bytes=64)
            scales = pool.tile([P, full], U8, name=tag + "s", tag=tag + "s", bufs=bufs, align_bytes=64)
            nc.vector.quantize_mx(
                out=codes[:, 0:width].bitcast(FP8X4), scales=scales[:, 0:width], in_=src
            )
            return (codes, scales)

        def quantise_x(u):
            n = units[u][2]
            xq[u] = quantise(xg[u][:, 0 : PACK * n], n, TOK, "xq", 3, ring)

        def alloc_wg(e):
            wg[e] = ring.tile([P, PACK * H], BF16, name="wg", tag="wg", bufs=2, align_bytes=64)

        def regroup_w3(e, c0=0, c1=H, engine="vector"):
            dst = wg[e][:, PACK * c0 : PACK * c1].rearrange("p (c i t) -> p c t i", i=RUN, t=PACK)
            src = w3_raw[e][:, :, c0:c1].rearrange("p t (c i) -> p c t i", i=RUN)
            if engine == "scalar":
                nc.scalar.copy(out=dst, in_=src)
            else:
                nc.vector.tensor_copy(out=dst, in_=src)

        def regroup_w4(e):
            w4g[e] = ring.tile([P, PACK * D], BF16, name="w4g", tag="w4g", bufs=2, align_bytes=64)
            dst = w4g[e][:].rearrange("p (c i t) -> p c t i", i=RUN, t=PACK)
            src = w4_raw[e][:].rearrange("p t (c i) -> p c t i", i=RUN)
            nc.vector.tensor_copy(out=dst, in_=src)

        pe_bank = {}

        def interleave(key, raw, c0, c1):
            bank = ps_w.tile([P, 2 * TOK], BF16, name="w", tag="w")
            for j in range((c1 - c0) // P):
                nc.tensor.matmul(
                    out=bank[:, TOK * j : TOK * j + TOK].rearrange("p (c i t) -> p c t i", i=RUN, t=PACK),
                    lhsT=ident_b[:],
                    rhs=raw[:, :, c0 + P * j : c0 + P * j + P].rearrange("p t (c i) -> p c t i", i=RUN),
                    start=True,
                    stop=True,
                )
            pe_bank[key] = bank

        def empty_w4(e):
            w4g[e] = ring.tile([P, PACK * D], BF16, name="w4g", tag="w4g", bufs=2, align_bytes=64)
            nc.scalar.copy(out=w4g[e][:], in_=pe_bank[("w4", e)][:, 0 : PACK * D])

        def empty_w3(e):
            c0 = H - PE_COLS
            nc.scalar.copy(out=wg[e][:, PACK * c0 :], in_=pe_bank[("w3", e)][:, 0 : PACK * PE_COLS])

        def quantise_w3(e, c0=0, c1=H):
            if e not in wq:
                wq[e] = (
                    keep.tile([P, H], U32, name="wqc%d" % e, align_bytes=64),
                    keep.tile([P, H], U8, name="wqs%d" % e, align_bytes=64),
                )
            codes, scales = wq[e]
            nc.vector.quantize_mx(
                out=codes[:, c0:c1].bitcast(FP8X4), scales=scales[:, c0:c1], in_=wg[e][:, PACK * c0 : PACK * c1]
            )

        def quantise_w4(e):
            w4q[e] = quantise(w4g[e][:], D, D, "w4q%d" % e, 1, keep)

        def layer1(u, m):
            e, t0, n = units[u]
            share = TOK // n
            if m % share == 0:
                zb[u] = ps_z.tile([P, TOK], F32, name="z", tag="z")
            z = zb[u][:, n * (m % share) : n * (m % share) + n]
            wc, ws = wq[e]
            xc, xs = xq[u]
            nc.tensor.matmul_mx(
                out=z,
                lhsT=wc[:, P * m : P * m + P].bitcast(FP8X4),
                lhsT_scale=ws[:, P * m : P * m + P],
                rhs=xc[:, 0:n].bitcast(FP8X4),
                rhs_scale=xs[:, 0:n],
                start=True,
                stop=True,
            )
            zt[(u, m)] = z

        def swish(u, m):
            e, t0, n = units[u]
            if m == 0:
                hr[u] = ring.tile([P, PACK, TOK], BF16, name="hr", tag="hr", bufs=3)
            col = PACK * e + m
            nc.scalar.activation(
                out=hr[u][:, m, 0:n],
                in_=zt[(u, m)],
                func=SILU,
                bias=b3_t[:, col : col + 1],
                scale=1.0,
            )

        def regroup_h(u):
            n = units[u][2]
            hg[u] = ring.tile([P, PACK * TOK], BF16, name="hg", tag="hg", bufs=2, align_bytes=64)
            cut = n - (P if u >= n_units - SHARE_H else 0)
            for engine, c0, c1 in (("vector", 0, cut), ("scalar", cut, n)):
                if c0 < c1:
                    dst = hg[u][:, PACK * c0 : PACK * c1].rearrange("p (c i t) -> p c t i", i=RUN, t=PACK)
                    src = hr[u][:, :, c0:c1].rearrange("p t (c i) -> p c t i", i=RUN)
                    if engine == "scalar":
                        nc.scalar.copy(out=dst, in_=src)
                    else:
                        nc.vector.tensor_copy(out=dst, in_=src)

        def quantise_h(u):
            n = units[u][2]
            hq[u] = quantise(hg[u][:, 0 : PACK * n], n, TOK, "hq", 3, ring)

        def layer2(u):
            e, t0, n = units[u]
            if u >= n_units - LATE_F and u % 2:
                o = ps_w.tile([P, TOK // P, D], F32, name="w", tag="w")
            else:
                o = ps_o.tile([P, TOK // P, D], F32, name="o", tag="o")
            hc, hs = hq[u]
            wc, ws = w4q[e]
            for c in range(n // P):
                nc.tensor.matmul_mx(
                    out=o[:, c, :],
                    lhsT=hc[:, P * c : P * c + P].bitcast(FP8X4),
                    lhsT_scale=hs[:, P * c : P * c + P],
                    rhs=wc[:].bitcast(FP8X4),
                    rhs_scale=ws[:],
                    start=True,
                    stop=True,
                )
            ot[u] = o

        def finish(u):
            e, t0, n = units[u]
            nch = n // P
            res = ring.tile([P, TOK // P, D], F32, name="res", tag="res", bufs=8)
            parts = [(c, c + 1) for c in range(nch)] if u == n_units - 1 else [(0, nch)]
            for c0, c1 in parts:
                nc.vector.tensor_tensor(
                    out=res[:, c0:c1, :],
                    in0=ot[u][:, c0:c1, :],
                    in1=b4_all[:, D * e : D * e + D].unsqueeze(1).to_broadcast([P, c1 - c0, D]),
                    op=ADD,
                )
                nc.sync.dma_start(
                    out=out_v[e, t0 + P * c0 : t0 + P * c1, :].rearrange("(c p) d -> p c d", p=P), in_=res[:, c0:c1, :]
                )

        wr_at = {}
        qw_at = {}
        w4_at = {}
        q4_at = {}
        for e in range(1, E):
            use = first_unit[e] - 1
            if e > 1:
                wr_at.setdefault(max(1, use - W_LEAD - 1), []).append(e)
            qw_at.setdefault(max(1, use - W_LEAD), []).append(e)
            w4_at.setdefault(use + W4_LATE, []).append(e)
            q4_at.setdefault(use + W4_LATE + 1, []).append(e)

        pe3_at = {}
        for e in range(PE_FROM, E):
            if PE_COLS:
                pe3_at.setdefault(first_unit[e] - 1 - W_LEAD - 1, []).append(e)

        alloc_wg(0)
        warm_up(2)
        transposes(0)
        evacuate(0)
        spread_b4()
        regroup_w3(0, 0, 256)
        nc.vector.tensor_copy(out=b3_f[:], in_=b3_rows[:])
        b3_ps = ps_t.tile([P, 4, P], F32, name="tp", tag="tp")
        nc.tensor.transpose(b3_ps[:, 0, :], b3_f[:], ident[:])
        quantise_w3(0, 0, 256)
        quantise_x(0)
        transposes(1)
        evacuate(1)
        layer1(0, 0)
        layer1(0, 1)
        regroup_w3(0, 256, 512)
        nc.vector.tensor_copy(out=b3_t[:], in_=b3_ps[:, 0, 0 : E * PACK])
        swish(0, 0)
        swish(0, 1)
        quantise_w3(0, 256, 512)
        quantise_x(1)
        layer1(0, 2)
        layer1(0, 3)
        for m in range(PACK):
            layer1(1, m)
            if m < 2:
                swish(0, m + 2)
        transposes(2)
        swish(1, 0)
        swish(1, 1)
        evacuate(2)
        alloc_wg(1)
        regroup_w3(1)
        transposes(3)

        ev_at = {}
        qx_at = {}
        for u in range(3, n_units):
            ev_at.setdefault(u - 3 if u >= n_units - AHEAD else u - 2, []).append(u)
        for u in range(2, n_units):
            qx_at.setdefault(u - 2 if u >= n_units - AHEAD else u - 1, []).append(u)
        fin_at = {}
        for u in range(n_units):
            fin_at.setdefault(u + 3 if u >= n_units - LATE_F else u + 2, []).append(u)

        for s in range(1, n_units + 3):
            if s <= n_units:
                regroup_h(s - 1)
            if s == 1:
                regroup_w4(0)
                quantise_h(0)
                quantise_w4(0)
            for u in qx_at.get(s, []):
                quantise_x(u)
            if s < n_units:
                for m in range(PACK):
                    if s > 1 or m > 1:
                        swish(s, m)
                    if s + 1 < n_units:
                        layer1(s + 1, m)
            for u in ev_at.get(s, []):
                evacuate(u)
            for e in w4_at.get(s, []):
                empty_w4(e)
            for e in pe3_at.get(s, []):
                empty_w3(e)
            for u in fin_at.get(s, []):
                finish(u)
            if s <= n_units:
                if s > 1:
                    quantise_h(s - 1)
                layer2(s - 1)
            for u in ev_at.get(s + 1, []):
                transposes(u)
            for e in wr_at.get(s, []):
                if e < PE_FROM:
                    alloc_wg(e)
                    regroup_w3(e)
                else:
                    regroup_w3(e, 0, H - PE_COLS)
            for e in w4_at.get(s + 1, []):
                interleave(("w4", e), w4_raw[e], 0, D)
            for e in pe3_at.get(s + 1, []):
                alloc_wg(e)
                interleave(("w3", e), w3_raw[e], H - PE_COLS, H)
            for e in qw_at.get(s, []):
                quantise_w3(e)
            for e in q4_at.get(s, []):
                quantise_w4(e)
